import numpy as np
import ml_dtypes


def mxq(x, axis, fmt="e4m3"):
    dtype, down = {"e4m3": (ml_dtypes.float8_e4m3fn, 7), "e5m2": (ml_dtypes.float8_e5m2, 14)}[fmt]
    v = np.moveaxis(np.asarray(x, np.float32).astype(ml_dtypes.bfloat16).astype(np.float64), axis, -1)
    blocks = v.reshape(v.shape[:-1] + (-1, 32))
    amax = np.abs(blocks).max(-1, keepdims=True)
    byte = np.maximum(np.where(amax > 0, np.frexp(amax)[1] - 1 + 127, 0) - down, 1)
    scale = np.exp2(byte - 127.0)
    codes = (blocks / scale).astype(np.float32).astype(dtype).astype(np.float64)
    return np.moveaxis((codes * scale).reshape(v.shape), -1, axis)


WIDE = False


def mx_kscale(k):
    if not WIDE:
        return np.ones(k)
    levels = np.array([10, -10, 5, -5, 0])
    a = np.random.permutation(np.resize(levels, k // 512 * 4)).reshape(k // 512, 4)
    idx = np.arange(k)
    return np.exp2(a[idx // 512, idx % 128 // 32])


BF16 = ml_dtypes.bfloat16


def bf(x):
    return np.asarray(x, np.float32).astype(BF16)


def f64(x):
    return np.asarray(x).astype(np.float64)


B, S, D, NH, NKV, HD, QB = 1, 512, 2048, 16, 4, 128, 512
Q_DIM = NH * HD
KV_DIM = NKV * HD


def rot(t, f0, f1):
    tp = t.reshape(t.shape[:-1] + (HD // 2, 2))
    t0, t1 = tp[..., 0], tp[..., 1]
    row1 = t0 * f0 + t1 * f1
    row0 = t0 * f1 - t1 * f0
    return np.stack([row0, row1], axis=-1).reshape(t.shape)


def setup_inputs():
    s = mx_kscale(D)
    return {"x": bf(np.random.standard_normal((B, S, D)) * s),
            "freqs_cis": bf(np.random.standard_normal((S, HD))),
            "Wqkv": bf(np.random.standard_normal((Q_DIM + 2 * KV_DIM, D)) / np.sqrt(D) / s)}


def reference(x, freqs_cis, Wqkv):
    xqkv = mxq(f64(x), 2, "e4m3") @ mxq(f64(Wqkv), 1, "e4m3").T
    xq = xqkv[..., :Q_DIM].reshape(B, S, NH, HD)
    xk = xqkv[..., Q_DIM:Q_DIM + KV_DIM].reshape(B, S, NKV, HD)
    xv = xqkv[..., Q_DIM + KV_DIM:].reshape(B, S, NKV, HD)
    f = f64(freqs_cis).reshape(S, 1, HD // 2, 2)
    f0, f1 = f[..., 0], f[..., 1]
    q_rot = rot(xq, f0, f1).transpose(0, 2, 1, 3)
    k_rot = rot(xk, f0, f1).transpose(0, 2, 1, 3)
    v = xv.transpose(0, 2, 1, 3)
    return q_rot, k_rot, v

@@ -1,0 +1,179 @@
+from contextlib import ExitStack
+
+import concourse.mybir as mybir
+from concourse.masks import make_identity
+
+F32 = mybir.dt.float32
+BF16 = mybir.dt.bfloat16
+U32 = mybir.dt.uint32
+U8 = mybir.dt.uint8
+FP8X4 = mybir.dt.float8_e4m3fn_x4
+MULT = mybir.AluOpType.mult
+ADD = mybir.AluOpType.add
+
+P = 128
+POSITIONS = 512
+K = 2048
+HEAD = 128
+PAIRS = HEAD // 2
+Q_HEADS, K_HEADS, V_HEADS = 16, 4, 4
+
+K_PASS = 4 * P
+PASSES = K // K_PASS
+WORDS = K_PASS // 2
+
+CHUNK = 512
+HALF = CHUNK // 2
+TILES = CHUNK // P
+CHUNK_HEADS = CHUNK // HEAD
+W_CHUNKS = (Q_HEADS + K_HEADS + V_HEADS) // CHUNK_HEADS
+ROTATED_CHUNKS = (Q_HEADS + K_HEADS) // CHUNK_HEADS
+W_CHUNKS_IN_SBUF = 4
+
+FLOPS = 2 * POSITIONS * K * (Q_HEADS + K_HEADS + V_HEADS) * HEAD
+
+
+def tile_rlaattention_pa_kernel(tc, x, freqs_cis, Wqkv, out_0, out_1, out_2):
+    nc = tc.nc
+
+    x_rows = x.flatten_outer_dims().rearrange("(p i) k -> p i k", i=TILES)
+    freq_rows = freqs_cis.rearrange("(p i) d -> p i d", i=TILES)
+    q_rows = out_0.rearrange("b h (p i) d -> p (b h) (i d)", i=TILES)
+    k_rows = out_1.rearrange("b h (p i) d -> p (b h) (i d)", i=TILES)
+    v_rows = out_2.rearrange("b h (p i) d -> p (b h) (i d)", i=TILES)
+    chunk_rows = [
+        q_rows[:, CHUNK_HEADS * n : CHUNK_HEADS * (n + 1), :]
+        for n in range(Q_HEADS // CHUNK_HEADS)
+    ] + [k_rows, v_rows]
+
+    with ExitStack() as ctx:
+        ctx.enter_context(tc.manual_schedule())
+        keep = ctx.enter_context(tc.tile_pool(name="keep", bufs=1))
+        raw_pool = ctx.enter_context(tc.tile_pool(name="raw", bufs=2 * W_CHUNKS_IN_SBUF))
+        stage = ctx.enter_context(tc.tile_pool(name="stage", bufs=4))
+        w_mx = ctx.enter_context(tc.tile_pool(name="w_mx", bufs=3))
+        work = ctx.enter_context(tc.tile_pool(name="work", bufs=3))
+        flipped_banks = ctx.enter_context(tc.psum_pool(name="flipped_banks", bufs=4))
+        sum_banks = ctx.enter_context(tc.psum_pool(name="sum_banks", bufs=4))
+
+        def load_w_chunk(n):
+            halves = []
+            for half in range(2):
+                first = CHUNK * n + HALF * half
+                w_raw = raw_pool.tile([P, HALF // P, K], BF16, tag="w_raw")
+                nc.sync.dma_start(
+                    out=w_raw[:],
+                    in_=Wqkv[first : first + HALF, :].rearrange("(r p) k -> p r k", p=P),
+                )
+                halves.append(w_raw)
+            return halves
+
+        def quantise_chunk(halves, codes, scales):
+            for half, raw in enumerate(halves):
+                rows = slice(HALF * half, HALF * (half + 1))
+                for c in range(PASSES):
+                    flipped = flipped_banks.tile([P, 2, HALF], F32, tag="flipped")
+                    for u in range(2):
+                        for r in range(HALF // P):
+                            first_word = WORDS * c + P * u
+                            nc.tensor.transpose(
+                                flipped[:, u, P * r : P * (r + 1)],
+                                raw[:, r, :].bitcast(F32)[:, first_word : first_word + P],
+                                identity[:],
+                            )
+                    grouped = stage.tile([P, 4 * HALF], BF16, tag="grouped", align_bytes=64)
+                    nc.scalar.copy(
+                        out=grouped[:].bitcast(F32).rearrange("p (n u) -> p n u", u=2),
+                        in_=flipped[:].rearrange("p u n -> p n u"),
+                    )
+                    nc.vector.quantize_mx(
+                        out=codes[:, c, rows].bitcast(FP8X4),
+                        scales=scales[:, c, rows],
+                        in_=grouped[:],
+                    )
+
+        freq_raw = keep.tile([P, TILES, PAIRS, 2], BF16)
+        nc.scalar.dma_start(
+            out=freq_raw[:].rearrange("p i j e -> p i (j e)"), in_=freq_rows
+        )
+        x_halves = []
+        for half in range(2):
+            x_raw = keep.tile([P, HALF // P, K], BF16, name="x_raw%d" % half)
+            nc.sync.dma_start(out=x_raw[:], in_=x_rows[:, 2 * half : 2 * half + 2, :])
+            x_halves.append(x_raw)
+        w_halves = [load_w_chunk(n) for n in range(W_CHUNKS_IN_SBUF)]
+
+        identity = keep.tile([P, P], F32)
+        make_identity(nc, identity[:])
+
+        for_even = keep.tile([P, TILES, PAIRS, 2], F32)
+        for_odd = keep.tile([P, TILES, PAIRS, 2], F32)
+        nc.vector.tensor_copy(out=for_even[:, :, :, 0], in_=freq_raw[:, :, :, 1])
+        nc.vector.tensor_copy(out=for_even[:, :, :, 1], in_=freq_raw[:, :, :, 0])
+        nc.vector.tensor_scalar_mul(for_odd[:, :, :, 0], freq_raw[:, :, :, 0], -1.0)
+        nc.vector.tensor_copy(out=for_odd[:, :, :, 1], in_=freq_raw[:, :, :, 1])
+
+        x_codes = keep.tile([P, PASSES, POSITIONS], U32, align_bytes=64)
+        x_scales = keep.tile([P, PASSES, POSITIONS], U8, align_bytes=64)
+        quantise_chunk(x_halves, x_codes, x_scales)
+
+        def prepare_w_chunk(n):
+            w_codes = w_mx.tile([P, PASSES, CHUNK], U32, tag="w_codes", align_bytes=64)
+            w_scales = w_mx.tile([P, PASSES, CHUNK], U8, tag="w_scales", align_bytes=64)
+            quantise_chunk(w_halves[n], w_codes, w_scales)
+            if n + W_CHUNKS_IN_SBUF < W_CHUNKS:
+                w_halves.append(load_w_chunk(n + W_CHUNKS_IN_SBUF))
+            return w_codes, w_scales
+
+        by_pair = [P, CHUNK_HEADS, PAIRS, 2]
+        prepared = prepare_w_chunk(0)
+        for n in range(W_CHUNKS):
+            w_codes, w_scales = prepared
+            if n + 1 < W_CHUNKS:
+                prepared = prepare_w_chunk(n + 1)
+
+            result = work.tile([P, CHUNK_HEADS, TILES, HEAD], F32, tag="result")
+            for i in range(TILES):
+                positions = slice(P * i, P * (i + 1))
+                sums = sum_banks.tile([P, CHUNK], F32, tag="sums")
+                for c in range(PASSES):
+                    nc.tensor.matmul_mx(
+                        out=sums[:],
+                        lhsT=x_codes[:, c, positions].bitcast(FP8X4),
+                        lhsT_scale=x_scales[:, c, positions],
+                        rhs=w_codes[:, c, :].bitcast(FP8X4),
+                        rhs_scale=w_scales[:, c, :],
+                        start=(c == 0),
+                        stop=(c == PASSES - 1),
+                    )
+                if n < ROTATED_CHUNKS:
+                    pairs = sums[:].rearrange("p (h j e) -> p h j e", h=CHUNK_HEADS, e=2)
+                    from_even = work.tile(by_pair, F32, tag="from_even")
+                    from_odd = work.tile(by_pair, F32, tag="from_odd")
+                    nc.vector.tensor_tensor(
+                        out=from_even[:],
+                        in0=pairs[:, :, :, 0:1].to_broadcast(by_pair),
+                        in1=for_even[:, i].unsqueeze(1).to_broadcast(by_pair),
+                        op=MULT,
+                    )
+                    nc.vector.tensor_tensor(
+                        out=from_odd[:],
+                        in0=pairs[:, :, :, 1:2].to_broadcast(by_pair),
+                        in1=for_odd[:, i].unsqueeze(1).to_broadcast(by_pair),
+                        op=MULT,
+                    )
+                    nc.gpsimd.tensor_tensor(
+                        out=result[:, :, i, :],
+                        in0=from_even[:].rearrange("p h j e -> p h (j e)"),
+                        in1=from_odd[:].rearrange("p h j e -> p h (j e)"),
+                        op=ADD,
+                    )
+                else:
+                    heads = sums[:].rearrange("p (h d) -> p h d", h=CHUNK_HEADS)
+                    if i % 2 == 0:
+                        nc.scalar.copy(out=result[:, :, i, :], in_=heads)
+                    else:
+                        nc.vector.tensor_copy(out=result[:, :, i, :], in_=heads)
+            nc.sync.dma_start(
+                out=chunk_rows[n], in_=result[:].rearrange("p h i d -> p h (i d)")
+            )

@@ -24,11 +24,13 @@ WORDS = K_PASS // 2
 
 CHUNK = 512
 HALF = CHUNK // 2
-TILES = CHUNK // P
+TILES = POSITIONS // P
 CHUNK_HEADS = CHUNK // HEAD
 W_CHUNKS = (Q_HEADS + K_HEADS + V_HEADS) // CHUNK_HEADS
+W_HALVES = 2 * W_CHUNKS
 ROTATED_CHUNKS = (Q_HEADS + K_HEADS) // CHUNK_HEADS
-W_CHUNKS_IN_SBUF = 4
+RAW_HALVES_IN_SBUF = 8
+HALVES_AHEAD = 2
 
 FLOPS = 2 * POSITIONS * K * (Q_HEADS + K_HEADS + V_HEADS) * HEAD
 
@@ -38,59 +40,53 @@ def tile_rlaattention_pa_kernel(tc, x, freqs_cis, Wqkv, out_0, out_1, out_2):
 
     x_rows = x.flatten_outer_dims().rearrange("(p i) k -> p i k", i=TILES)
     freq_rows = freqs_cis.rearrange("(p i) d -> p i d", i=TILES)
-    q_rows = out_0.rearrange("b h (p i) d -> p (b h) (i d)", i=TILES)
-    k_rows = out_1.rearrange("b h (p i) d -> p (b h) (i d)", i=TILES)
-    v_rows = out_2.rearrange("b h (p i) d -> p (b h) (i d)", i=TILES)
+    q_rows = out_0.rearrange("b h (p i) d -> p (b h) i d", i=TILES)
+    k_rows = out_1.rearrange("b h (p i) d -> p (b h) i d", i=TILES)
+    v_rows = out_2.rearrange("b h (p i) d -> p (b h) i d", i=TILES)
     chunk_rows = [
-        q_rows[:, CHUNK_HEADS * n : CHUNK_HEADS * (n + 1), :]
+        q_rows[:, CHUNK_HEADS * n : CHUNK_HEADS * (n + 1)]
         for n in range(Q_HEADS // CHUNK_HEADS)
     ] + [k_rows, v_rows]
 
     with ExitStack() as ctx:
         ctx.enter_context(tc.manual_schedule())
         keep = ctx.enter_context(tc.tile_pool(name="keep", bufs=1))
-        raw_pool = ctx.enter_context(tc.tile_pool(name="raw", bufs=2 * W_CHUNKS_IN_SBUF))
-        stage = ctx.enter_context(tc.tile_pool(name="stage", bufs=4))
+        raw_pool = ctx.enter_context(tc.tile_pool(name="raw", bufs=RAW_HALVES_IN_SBUF))
+        stage = ctx.enter_context(tc.tile_pool(name="stage", bufs=2 * PASSES))
         w_mx = ctx.enter_context(tc.tile_pool(name="w_mx", bufs=3))
-        work = ctx.enter_context(tc.tile_pool(name="work", bufs=3))
+        work = ctx.enter_context(tc.tile_pool(name="work", bufs=4))
         flipped_banks = ctx.enter_context(tc.psum_pool(name="flipped_banks", bufs=4))
         sum_banks = ctx.enter_context(tc.psum_pool(name="sum_banks", bufs=4))
 
-        def load_w_chunk(n):
-            halves = []
-            for half in range(2):
-                first = CHUNK * n + HALF * half
-                w_raw = raw_pool.tile([P, HALF // P, K], BF16, tag="w_raw")
-                nc.sync.dma_start(
-                    out=w_raw[:],
-                    in_=Wqkv[first : first + HALF, :].rearrange("(r p) k -> p r k", p=P),
-                )
-                halves.append(w_raw)
-            return halves
+        def load_w_half(h):
+            w_raw = raw_pool.tile([P, HALF // P, K], BF16, tag="w_raw")
+            nc.sync.dma_start(
+                out=w_raw[:],
+                in_=Wqkv[HALF * h : HALF * (h + 1), :].rearrange("(r p) k -> p r k", p=P),
+            )
+            return w_raw
 
-        def quantise_chunk(halves, codes, scales):
-            for half, raw in enumerate(halves):
-                rows = slice(HALF * half, HALF * (half + 1))
-                for c in range(PASSES):
-                    flipped = flipped_banks.tile([P, 2, HALF], F32, tag="flipped")
-                    for u in range(2):
-                        for r in range(HALF // P):
-                            first_word = WORDS * c + P * u
-                            nc.tensor.transpose(
-                                flipped[:, u, P * r : P * (r + 1)],
-                                raw[:, r, :].bitcast(F32)[:, first_word : first_word + P],
-                                identity[:],
-                            )
-                    grouped = stage.tile([P, 4 * HALF], BF16, tag="grouped", align_bytes=64)
-                    nc.scalar.copy(
-                        out=grouped[:].bitcast(F32).rearrange("p (n u) -> p n u", u=2),
-                        in_=flipped[:].rearrange("p u n -> p n u"),
-                    )
-                    nc.vector.quantize_mx(
-                        out=codes[:, c, rows].bitcast(FP8X4),
-                        scales=scales[:, c, rows],
-                        in_=grouped[:],
-                    )
+        def quantise_half(raw, codes, scales, rows):
+            for c in range(PASSES):
+                flipped = flipped_banks.tile([P, 2, HALF], F32, tag="flipped")
+                for u in range(2):
+                    for r in range(HALF // P):
+                        first_word = WORDS * c + P * u
+                        nc.tensor.transpose(
+                            flipped[:, u, P * r : P * (r + 1)],
+                            raw[:, r, :].bitcast(F32)[:, first_word : first_word + P],
+                            identity[:],
+                        )
+                grouped = stage.tile([P, 4 * HALF], BF16, tag="grouped", align_bytes=64)
+                nc.scalar.copy(
+                    out=grouped[:].bitcast(F32).rearrange("p (n u) -> p n u", u=2),
+                    in_=flipped[:].rearrange("p u n -> p n u"),
+                )
+                nc.vector.quantize_mx(
+                    out=codes[:, c, rows].bitcast(FP8X4),
+                    scales=scales[:, c, rows],
+                    in_=grouped[:],
+                )
 
         freq_raw = keep.tile([P, TILES, PAIRS, 2], BF16)
         nc.scalar.dma_start(
@@ -101,7 +97,7 @@ def tile_rlaattention_pa_kernel(tc, x, freqs_cis, Wqkv, out_0, out_1, out_2):
             x_raw = keep.tile([P, HALF // P, K], BF16, name="x_raw%d" % half)
             nc.sync.dma_start(out=x_raw[:], in_=x_rows[:, 2 * half : 2 * half + 2, :])
             x_halves.append(x_raw)
-        w_halves = [load_w_chunk(n) for n in range(W_CHUNKS_IN_SBUF)]
+        w_raws = [load_w_half(h) for h in range(RAW_HALVES_IN_SBUF)]
 
         identity = keep.tile([P, P], F32)
         make_identity(nc, identity[:])
@@ -115,25 +111,39 @@ def tile_rlaattention_pa_kernel(tc, x, freqs_cis, Wqkv, out_0, out_1, out_2):
 
         x_codes = keep.tile([P, PASSES, POSITIONS], U32, align_bytes=64)
         x_scales = keep.tile([P, PASSES, POSITIONS], U8, align_bytes=64)
-        quantise_chunk(x_halves, x_codes, x_scales)
+        for half in range(2):
+            quantise_half(
+                x_halves[half], x_codes, x_scales, slice(HALF * half, HALF * (half + 1))
+            )
 
-        def prepare_w_chunk(n):
-            w_codes = w_mx.tile([P, PASSES, CHUNK], U32, tag="w_codes", align_bytes=64)
-            w_scales = w_mx.tile([P, PASSES, CHUNK], U8, tag="w_scales", align_bytes=64)
-            quantise_chunk(w_halves[n], w_codes, w_scales)
-            if n + W_CHUNKS_IN_SBUF < W_CHUNKS:
-                w_halves.append(load_w_chunk(n + W_CHUNKS_IN_SBUF))
-            return w_codes, w_scales
+        w_quantised = []
+
+        def prepare_w_half(h):
+            if h % 2 == 0:
+                w_codes = w_mx.tile([P, PASSES, CHUNK], U32, tag="w_codes", align_bytes=64)
+                w_scales = w_mx.tile([P, PASSES, CHUNK], U8, tag="w_scales", align_bytes=64)
+                w_quantised.append((w_codes, w_scales))
+            codes, scales = w_quantised[h // 2]
+            quantise_half(
+                w_raws[h], codes, scales, slice(HALF * (h % 2), HALF * (h % 2 + 1))
+            )
+            if h + RAW_HALVES_IN_SBUF < W_HALVES:
+                w_raws.append(load_w_half(h + RAW_HALVES_IN_SBUF))
+
+        for h in range(HALVES_AHEAD):
+            prepare_w_half(h)
 
         by_pair = [P, CHUNK_HEADS, PAIRS, 2]
-        prepared = prepare_w_chunk(0)
-        for n in range(W_CHUNKS):
-            w_codes, w_scales = prepared
-            if n + 1 < W_CHUNKS:
-                prepared = prepare_w_chunk(n + 1)
+        for round_number in range(W_HALVES):
+            n = round_number // 2
+            first_tile = 2 * (round_number % 2)
+            if round_number + HALVES_AHEAD < W_HALVES:
+                prepare_w_half(round_number + HALVES_AHEAD)
+            w_codes, w_scales = w_quantised[n]
 
-            result = work.tile([P, CHUNK_HEADS, TILES, HEAD], F32, tag="result")
-            for i in range(TILES):
+            result = work.tile([P, CHUNK_HEADS, 2, HEAD], F32, tag="result")
+            for t in range(2):
+                i = first_tile + t
                 positions = slice(P * i, P * (i + 1))
                 sums = sum_banks.tile([P, CHUNK], F32, tag="sums")
                 for c in range(PASSES):
@@ -163,17 +173,17 @@ def tile_rlaattention_pa_kernel(tc, x, freqs_cis, Wqkv, out_0, out_1, out_2):
                         op=MULT,
                     )
                     nc.gpsimd.tensor_tensor(
-                        out=result[:, :, i, :],
+                        out=result[:, :, t, :],
                         in0=from_even[:].rearrange("p h j e -> p h (j e)"),
                         in1=from_odd[:].rearrange("p h j e -> p h (j e)"),
                         op=ADD,
                     )
                 else:
                     heads = sums[:].rearrange("p (h d) -> p h d", h=CHUNK_HEADS)
-                    if i % 2 == 0:
-                        nc.scalar.copy(out=result[:, :, i, :], in_=heads)
+                    if t == 0:
+                        nc.scalar.copy(out=result[:, :, t, :], in_=heads)
                     else:
-                        nc.vector.tensor_copy(out=result[:, :, i, :], in_=heads)
+                        nc.vector.tensor_copy(out=result[:, :, t, :], in_=heads)
             nc.sync.dma_start(
-                out=chunk_rows[n], in_=result[:].rearrange("p h i d -> p h (i d)")
+                out=chunk_rows[n][:, :, first_tile : first_tile + 2, :], in_=result[:]
             )

@@ -22,15 +22,14 @@ K_PASS = 4 * P
 PASSES = K // K_PASS
 WORDS = K_PASS // 2
 
-CHUNK = 512
-HALF = CHUNK // 2
+SLAB = 256
+SLAB_TILES = SLAB // P
+SLAB_HEADS = SLAB // HEAD
 TILES = POSITIONS // P
-CHUNK_HEADS = CHUNK // HEAD
-W_CHUNKS = (Q_HEADS + K_HEADS + V_HEADS) // CHUNK_HEADS
-W_HALVES = 2 * W_CHUNKS
-ROTATED_CHUNKS = (Q_HEADS + K_HEADS) // CHUNK_HEADS
-RAW_HALVES_IN_SBUF = 8
-HALVES_AHEAD = 2
+X_SLABS = POSITIONS // SLAB
+W_SLABS = (Q_HEADS + K_HEADS + V_HEADS) // SLAB_HEADS
+ROTATED_SLABS = (Q_HEADS + K_HEADS) // SLAB_HEADS
+RAW_SLABS_IN_SBUF = 8
 
 FLOPS = 2 * POSITIONS * K * (Q_HEADS + K_HEADS + V_HEADS) * HEAD
 
@@ -40,64 +39,65 @@ def tile_rlaattention_pa_kernel(tc, x, freqs_cis, Wqkv, out_0, out_1, out_2):
 
     x_rows = x.flatten_outer_dims().rearrange("(p i) k -> p i k", i=TILES)
     freq_rows = freqs_cis.rearrange("(p i) d -> p i d", i=TILES)
-    q_rows = out_0.rearrange("b h (p i) d -> p (b h) i d", i=TILES)
-    k_rows = out_1.rearrange("b h (p i) d -> p (b h) i d", i=TILES)
-    v_rows = out_2.rearrange("b h (p i) d -> p (b h) i d", i=TILES)
-    chunk_rows = [
-        q_rows[:, CHUNK_HEADS * n : CHUNK_HEADS * (n + 1)]
-        for n in range(Q_HEADS // CHUNK_HEADS)
-    ] + [k_rows, v_rows]
+    slab_rows = [
+        out.rearrange("b h (p i) d -> p (b h) i d", i=TILES)[:, h : h + SLAB_HEADS]
+        for out, heads in ((out_0, Q_HEADS), (out_1, K_HEADS), (out_2, V_HEADS))
+        for h in range(0, heads, SLAB_HEADS)
+    ]
 
     with ExitStack() as ctx:
         ctx.enter_context(tc.manual_schedule())
         keep = ctx.enter_context(tc.tile_pool(name="keep", bufs=1))
-        raw_pool = ctx.enter_context(tc.tile_pool(name="raw", bufs=RAW_HALVES_IN_SBUF))
+        raw_pool = ctx.enter_context(tc.tile_pool(name="raw", bufs=RAW_SLABS_IN_SBUF))
         stage = ctx.enter_context(tc.tile_pool(name="stage", bufs=2 * PASSES))
         w_mx = ctx.enter_context(tc.tile_pool(name="w_mx", bufs=3))
-        work = ctx.enter_context(tc.tile_pool(name="work", bufs=4))
+        products = ctx.enter_context(tc.tile_pool(name="products", bufs=4))
+        results = ctx.enter_context(tc.tile_pool(name="results", bufs=10))
         flipped_banks = ctx.enter_context(tc.psum_pool(name="flipped_banks", bufs=4))
         sum_banks = ctx.enter_context(tc.psum_pool(name="sum_banks", bufs=4))
 
-        def load_w_half(h):
-            w_raw = raw_pool.tile([P, HALF // P, K], BF16, tag="w_raw")
+        def load_w_slab(s):
+            w_raw = raw_pool.tile([P, SLAB_TILES, K], BF16, tag="w_raw")
             nc.sync.dma_start(
                 out=w_raw[:],
-                in_=Wqkv[HALF * h : HALF * (h + 1), :].rearrange("(r p) k -> p r k", p=P),
+                in_=Wqkv[SLAB * s : SLAB * (s + 1), :].rearrange("(r p) k -> p r k", p=P),
             )
             return w_raw
 
-        def quantise_half(raw, codes, scales, rows):
+        def quantise_slab(raw, codes, scales, vector_helps):
             for c in range(PASSES):
-                flipped = flipped_banks.tile([P, 2, HALF], F32, tag="flipped")
+                flipped = flipped_banks.tile([P, 2, SLAB], F32, tag="flipped")
                 for u in range(2):
-                    for r in range(HALF // P):
+                    for r in range(SLAB_TILES):
                         first_word = WORDS * c + P * u
                         nc.tensor.transpose(
                             flipped[:, u, P * r : P * (r + 1)],
                             raw[:, r, :].bitcast(F32)[:, first_word : first_word + P],
                             identity[:],
                         )
-                grouped = stage.tile([P, 4 * HALF], BF16, tag="grouped", align_bytes=64)
-                nc.scalar.copy(
-                    out=grouped[:].bitcast(F32).rearrange("p (n u) -> p n u", u=2),
-                    in_=flipped[:].rearrange("p u n -> p n u"),
-                )
+                grouped = stage.tile([P, 4 * SLAB], BF16, tag="grouped", align_bytes=64)
+                side_by_side = grouped[:].bitcast(F32).rearrange("p (n u) -> p n u", u=2)
+                planes = flipped[:].rearrange("p u n -> p n u")
+                if vector_helps and c == 1:
+                    nc.vector.tensor_copy(out=side_by_side, in_=planes)
+                else:
+                    nc.scalar.copy(out=side_by_side, in_=planes)
                 nc.vector.quantize_mx(
-                    out=codes[:, c, rows].bitcast(FP8X4),
-                    scales=scales[:, c, rows],
-                    in_=grouped[:],
+                    out=codes[:, c, :].bitcast(FP8X4), scales=scales[:, c, :], in_=grouped[:]
                 )
 
         freq_raw = keep.tile([P, TILES, PAIRS, 2], BF16)
         nc.scalar.dma_start(
             out=freq_raw[:].rearrange("p i j e -> p i (j e)"), in_=freq_rows
         )
-        x_halves = []
-        for half in range(2):
-            x_raw = keep.tile([P, HALF // P, K], BF16, name="x_raw%d" % half)
-            nc.sync.dma_start(out=x_raw[:], in_=x_rows[:, 2 * half : 2 * half + 2, :])
-            x_halves.append(x_raw)
-        w_raws = [load_w_half(h) for h in range(RAW_HALVES_IN_SBUF)]
+        x_raws = []
+        for s in range(X_SLABS):
+            x_raw = keep.tile([P, SLAB_TILES, K], BF16, name="x_raw%d" % s)
+            nc.sync.dma_start(
+                out=x_raw[:], in_=x_rows[:, SLAB_TILES * s : SLAB_TILES * (s + 1), :]
+            )
+            x_raws.append(x_raw)
+        w_raws = [load_w_slab(s) for s in range(RAW_SLABS_IN_SBUF)]
 
         identity = keep.tile([P, P], F32)
         make_identity(nc, identity[:])
@@ -111,79 +111,72 @@ def tile_rlaattention_pa_kernel(tc, x, freqs_cis, Wqkv, out_0, out_1, out_2):
 
         x_codes = keep.tile([P, PASSES, POSITIONS], U32, align_bytes=64)
         x_scales = keep.tile([P, PASSES, POSITIONS], U8, align_bytes=64)
-        for half in range(2):
-            quantise_half(
-                x_halves[half], x_codes, x_scales, slice(HALF * half, HALF * (half + 1))
-            )
+        for s in range(X_SLABS):
+            columns = slice(SLAB * s, SLAB * (s + 1))
+            quantise_slab(x_raws[s], x_codes[:, :, columns], x_scales[:, :, columns], True)
 
-        w_quantised = []
+        def prepare_w_slab(s):
+            w_codes = w_mx.tile([P, PASSES, SLAB], U32, tag="w_codes", align_bytes=64)
+            w_scales = w_mx.tile([P, PASSES, SLAB], U8, tag="w_scales", align_bytes=64)
+            quantise_slab(w_raws[s], w_codes, w_scales, s <= 1)
+            if s + RAW_SLABS_IN_SBUF < W_SLABS:
+                w_raws.append(load_w_slab(s + RAW_SLABS_IN_SBUF))
+            return w_codes, w_scales
 
-        def prepare_w_half(h):
-            if h % 2 == 0:
-                w_codes = w_mx.tile([P, PASSES, CHUNK], U32, tag="w_codes", align_bytes=64)
-                w_scales = w_mx.tile([P, PASSES, CHUNK], U8, tag="w_scales", align_bytes=64)
-                w_quantised.append((w_codes, w_scales))
-            codes, scales = w_quantised[h // 2]
-            quantise_half(
-                w_raws[h], codes, scales, slice(HALF * (h % 2), HALF * (h % 2 + 1))
-            )
-            if h + RAW_HALVES_IN_SBUF < W_HALVES:
-                w_raws.append(load_w_half(h + RAW_HALVES_IN_SBUF))
+        by_member = [P, 2, SLAB_HEADS, PAIRS, 2]
+        prepared = prepare_w_slab(0)
+        for s in range(W_SLABS):
+            w_codes, w_scales = prepared
+            if s + 1 < W_SLABS:
+                prepared = prepare_w_slab(s + 1)
 
-        for h in range(HALVES_AHEAD):
-            prepare_w_half(h)
-
-        by_pair = [P, CHUNK_HEADS, PAIRS, 2]
-        for round_number in range(W_HALVES):
-            n = round_number // 2
-            first_tile = 2 * (round_number % 2)
-            if round_number + HALVES_AHEAD < W_HALVES:
-                prepare_w_half(round_number + HALVES_AHEAD)
-            w_codes, w_scales = w_quantised[n]
-
-            result = work.tile([P, CHUNK_HEADS, 2, HEAD], F32, tag="result")
-            for t in range(2):
-                i = first_tile + t
-                positions = slice(P * i, P * (i + 1))
-                sums = sum_banks.tile([P, CHUNK], F32, tag="sums")
-                for c in range(PASSES):
-                    nc.tensor.matmul_mx(
-                        out=sums[:],
-                        lhsT=x_codes[:, c, positions].bitcast(FP8X4),
-                        lhsT_scale=x_scales[:, c, positions],
-                        rhs=w_codes[:, c, :].bitcast(FP8X4),
-                        rhs_scale=w_scales[:, c, :],
-                        start=(c == 0),
-                        stop=(c == PASSES - 1),
+            for first_tile in range(0, TILES, 2):
+                sums = sum_banks.tile([P, 2, SLAB], F32, tag="sums")
+                for t in range(2):
+                    positions = slice(P * (first_tile + t), P * (first_tile + t + 1))
+                    for c in range(PASSES):
+                        nc.tensor.matmul_mx(
+                            out=sums[:, t, :],
+                            lhsT=x_codes[:, c, positions].bitcast(FP8X4),
+                            lhsT_scale=x_scales[:, c, positions],
+                            rhs=w_codes[:, c, :].bitcast(FP8X4),
+                            rhs_scale=w_scales[:, c, :],
+                            start=(c == 0),
+                            stop=(c == PASSES - 1),
+                        )
+                result = results.tile([P, SLAB_HEADS, 2, HEAD], F32, tag="result")
+                result_by_tile = result[:].rearrange("p h t d -> p t h d")
+                if s < ROTATED_SLABS:
+                    members = sums[:].rearrange(
+                        "p t (h j e) -> p t h j e", h=SLAB_HEADS, e=2
                     )
-                if n < ROTATED_CHUNKS:
-                    pairs = sums[:].rearrange("p (h j e) -> p h j e", h=CHUNK_HEADS, e=2)
-                    from_even = work.tile(by_pair, F32, tag="from_even")
-                    from_odd = work.tile(by_pair, F32, tag="from_odd")
+                    tiles = slice(first_tile, first_tile + 2)
+                    from_even = products.tile(by_member, F32, tag="from_even")
+                    from_odd = products.tile(by_member, F32, tag="from_odd")
                     nc.vector.tensor_tensor(
                         out=from_even[:],
-                        in0=pairs[:, :, :, 0:1].to_broadcast(by_pair),
-                        in1=for_even[:, i].unsqueeze(1).to_broadcast(by_pair),
+                        in0=members[:, :, :, :, 0:1].to_broadcast(by_member),
+                        in1=for_even[:, tiles].unsqueeze(2).to_broadcast(by_member),
                         op=MULT,
                     )
                     nc.vector.tensor_tensor(
                         out=from_odd[:],
-                        in0=pairs[:, :, :, 1:2].to_broadcast(by_pair),
-                        in1=for_odd[:, i].unsqueeze(1).to_broadcast(by_pair),
+                        in0=members[:, :, :, :, 1:2].to_broadcast(by_member),
+                        in1=for_odd[:, tiles].unsqueeze(2).to_broadcast(by_member),
                         op=MULT,
                     )
                     nc.gpsimd.tensor_tensor(
-                        out=result[:, :, t, :],
-                        in0=from_even[:].rearrange("p h j e -> p h (j e)"),
-                        in1=from_odd[:].rearrange("p h j e -> p h (j e)"),
+                        out=result_by_tile,
+                        in0=from_even[:].rearrange("p t h j e -> p t h (j e)"),
+                        in1=from_odd[:].rearrange("p t h j e -> p t h (j e)"),
                         op=ADD,
                     )
                 else:
-                    heads = sums[:].rearrange("p (h d) -> p h d", h=CHUNK_HEADS)
-                    if t == 0:
-                        nc.scalar.copy(out=result[:, :, t, :], in_=heads)
+                    sums_by_head = sums[:].rearrange("p t (h d) -> p t h d", h=SLAB_HEADS)
+                    if first_tile == 0:
+                        nc.scalar.copy(out=result_by_tile, in_=sums_by_head)
                     else:
-                        nc.vector.tensor_copy(out=result[:, :, t, :], in_=heads)
-            nc.sync.dma_start(
-                out=chunk_rows[n][:, :, first_tile : first_tile + 2, :], in_=result[:]
-            )
+                        nc.vector.tensor_copy(out=result_by_tile, in_=sums_by_head)
+                nc.sync.dma_start(
+                    out=slab_rows[s][:, :, first_tile : first_tile + 2, :], in_=result[:]
+                )

@@ -51,8 +51,8 @@ def tile_rlaattention_pa_kernel(tc, x, freqs_cis, Wqkv, out_0, out_1, out_2):
         raw_pool = ctx.enter_context(tc.tile_pool(name="raw", bufs=RAW_SLABS_IN_SBUF))
         stage = ctx.enter_context(tc.tile_pool(name="stage", bufs=2 * PASSES))
         w_mx = ctx.enter_context(tc.tile_pool(name="w_mx", bufs=3))
-        products = ctx.enter_context(tc.tile_pool(name="products", bufs=4))
-        results = ctx.enter_context(tc.tile_pool(name="results", bufs=10))
+        products = ctx.enter_context(tc.tile_pool(name="products", bufs=3))
+        results = ctx.enter_context(tc.tile_pool(name="results", bufs=8))
         flipped_banks = ctx.enter_context(tc.psum_pool(name="flipped_banks", bufs=4))
         sum_banks = ctx.enter_context(tc.psum_pool(name="sum_banks", bufs=4))
 
@@ -64,7 +64,8 @@ def tile_rlaattention_pa_kernel(tc, x, freqs_cis, Wqkv, out_0, out_1, out_2):
             )
             return w_raw
 
-        def quantise_slab(raw, codes, scales, vector_helps):
+        def flip_slab(raw, vector_helps):
+            grouped_tiles = []
             for c in range(PASSES):
                 flipped = flipped_banks.tile([P, 2, SLAB], F32, tag="flipped")
                 for u in range(2):
@@ -82,8 +83,15 @@ def tile_rlaattention_pa_kernel(tc, x, freqs_cis, Wqkv, out_0, out_1, out_2):
                     nc.vector.tensor_copy(out=side_by_side, in_=planes)
                 else:
                     nc.scalar.copy(out=side_by_side, in_=planes)
+                grouped_tiles.append(grouped)
+            return grouped_tiles
+
+        def quantise_slab(grouped_tiles, codes, scales):
+            for c in range(PASSES):
                 nc.vector.quantize_mx(
-                    out=codes[:, c, :].bitcast(FP8X4), scales=scales[:, c, :], in_=grouped[:]
+                    out=codes[:, c, :].bitcast(FP8X4),
+                    scales=scales[:, c, :],
+                    in_=grouped_tiles[c][:],
                 )
 
         freq_raw = keep.tile([P, TILES, PAIRS, 2], BF16)
@@ -113,70 +121,88 @@ def tile_rlaattention_pa_kernel(tc, x, freqs_cis, Wqkv, out_0, out_1, out_2):
         x_scales = keep.tile([P, PASSES, POSITIONS], U8, align_bytes=64)
         for s in range(X_SLABS):
             columns = slice(SLAB * s, SLAB * (s + 1))
-            quantise_slab(x_raws[s], x_codes[:, :, columns], x_scales[:, :, columns], True)
+            quantise_slab(
+                flip_slab(x_raws[s], True), x_codes[:, :, columns], x_scales[:, :, columns]
+            )
 
-        def prepare_w_slab(s):
-            w_codes = w_mx.tile([P, PASSES, SLAB], U32, tag="w_codes", align_bytes=64)
-            w_scales = w_mx.tile([P, PASSES, SLAB], U8, tag="w_scales", align_bytes=64)
-            quantise_slab(w_raws[s], w_codes, w_scales, s <= 1)
+        w_grouped = []
+        w_quantised = []
+
+        def flip_w_slab(s):
+            w_grouped.append(flip_slab(w_raws[s], s < 2))
             if s + RAW_SLABS_IN_SBUF < W_SLABS:
                 w_raws.append(load_w_slab(s + RAW_SLABS_IN_SBUF))
-            return w_codes, w_scales
 
+        def quantise_w_slab(s):
+            w_codes = w_mx.tile([P, PASSES, SLAB], U32, tag="w_codes", align_bytes=64)
+            w_scales = w_mx.tile([P, PASSES, SLAB], U8, tag="w_scales", align_bytes=64)
+            quantise_slab(w_grouped[s], w_codes, w_scales)
+            w_quantised.append((w_codes, w_scales))
+
+        def multiply_slab(s, first_tile):
+            w_codes, w_scales = w_quantised[s]
+            sums = sum_banks.tile([P, 2, SLAB], F32, tag="sums")
+            for t in range(2):
+                positions = slice(P * (first_tile + t), P * (first_tile + t + 1))
+                for c in range(PASSES):
+                    nc.tensor.matmul_mx(
+                        out=sums[:, t, :],
+                        lhsT=x_codes[:, c, positions].bitcast(FP8X4),
+                        lhsT_scale=x_scales[:, c, positions],
+                        rhs=w_codes[:, c, :].bitcast(FP8X4),
+                        rhs_scale=w_scales[:, c, :],
+                        start=(c == 0),
+                        stop=(c == PASSES - 1),
+                    )
+            return sums
+
+        flip_w_slab(0)
+        quantise_w_slab(0)
+        flip_w_slab(1)
         by_member = [P, 2, SLAB_HEADS, PAIRS, 2]
-        prepared = prepare_w_slab(0)
         for s in range(W_SLABS):
-            w_codes, w_scales = prepared
+            if s + 2 < W_SLABS:
+                flip_w_slab(s + 2)
             if s + 1 < W_SLABS:
-                prepared = prepare_w_slab(s + 1)
+                quantise_w_slab(s + 1)
 
-            for first_tile in range(0, TILES, 2):
-                sums = sum_banks.tile([P, 2, SLAB], F32, tag="sums")
-                for t in range(2):
-                    positions = slice(P * (first_tile + t), P * (first_tile + t + 1))
-                    for c in range(PASSES):
-                        nc.tensor.matmul_mx(
-                            out=sums[:, t, :],
-                            lhsT=x_codes[:, c, positions].bitcast(FP8X4),
-                            lhsT_scale=x_scales[:, c, positions],
-                            rhs=w_codes[:, c, :].bitcast(FP8X4),
-                            rhs_scale=w_scales[:, c, :],
-                            start=(c == 0),
-                            stop=(c == PASSES - 1),
-                        )
-                result = results.tile([P, SLAB_HEADS, 2, HEAD], F32, tag="result")
-                result_by_tile = result[:].rearrange("p h t d -> p t h d")
-                if s < ROTATED_SLABS:
+            if s < ROTATED_SLABS:
+                from_even = products.tile([P, TILES, SLAB_HEADS, PAIRS, 2], F32, tag="from_even")
+                from_odd = products.tile([P, TILES, SLAB_HEADS, PAIRS, 2], F32, tag="from_odd")
+                for first_tile in range(0, TILES, 2):
+                    sums = multiply_slab(s, first_tile)
                     members = sums[:].rearrange(
                         "p t (h j e) -> p t h j e", h=SLAB_HEADS, e=2
                     )
                     tiles = slice(first_tile, first_tile + 2)
-                    from_even = products.tile(by_member, F32, tag="from_even")
-                    from_odd = products.tile(by_member, F32, tag="from_odd")
                     nc.vector.tensor_tensor(
-                        out=from_even[:],
+                        out=from_even[:, tiles],
                         in0=members[:, :, :, :, 0:1].to_broadcast(by_member),
                         in1=for_even[:, tiles].unsqueeze(2).to_broadcast(by_member),
                         op=MULT,
                     )
                     nc.vector.tensor_tensor(
-                        out=from_odd[:],
+                        out=from_odd[:, tiles],
                         in0=members[:, :, :, :, 1:2].to_broadcast(by_member),
                         in1=for_odd[:, tiles].unsqueeze(2).to_broadcast(by_member),
                         op=MULT,
                     )
-                    nc.gpsimd.tensor_tensor(
-                        out=result_by_tile,
-                        in0=from_even[:].rearrange("p t h j e -> p t h (j e)"),
-                        in1=from_odd[:].rearrange("p t h j e -> p t h (j e)"),
-                        op=ADD,
-                    )
-                else:
-                    sums_by_head = sums[:].rearrange("p t (h d) -> p t h d", h=SLAB_HEADS)
-                    if first_tile == 0:
-                        nc.scalar.copy(out=result_by_tile, in_=sums_by_head)
-                    else:
-                        nc.vector.tensor_copy(out=result_by_tile, in_=sums_by_head)
-                nc.sync.dma_start(
-                    out=slab_rows[s][:, :, first_tile : first_tile + 2, :], in_=result[:]
+                result = results.tile([P, SLAB_HEADS, TILES, HEAD], F32, tag="result")
+                nc.gpsimd.tensor_tensor(
+                    out=result[:].rearrange("p h i d -> p i h d"),
+                    in0=from_even[:].rearrange("p i h j e -> p i h (j e)"),
+                    in1=from_odd[:].rearrange("p i h j e -> p i h (j e)"),
+                    op=ADD,
                 )
+                nc.sync.dma_start(out=slab_rows[s], in_=result[:])
+            else:
+                for first_tile in range(0, TILES, 2):
+                    sums = multiply_slab(s, first_tile)
+                    values = results.tile([P, SLAB_HEADS, 2, HEAD], F32, tag="values")
+                    nc.scalar.copy(
+                        out=values[:].rearrange("p h t d -> p t h d"),
+                        in_=sums[:].rearrange("p t (h d) -> p t h d", h=SLAB_HEADS),
+                    )
+                    nc.scalar.dma_start(
+                        out=slab_rows[s][:, :, first_tile : first_tile + 2, :], in_=values[:]
+                    )

from contextlib import ExitStack

import concourse.mybir as mybir
from concourse.masks import make_identity

F32 = mybir.dt.float32
BF16 = mybir.dt.bfloat16
U32 = mybir.dt.uint32
U8 = mybir.dt.uint8
FP8X4 = mybir.dt.float8_e4m3fn_x4
MULT = mybir.AluOpType.mult
ADD = mybir.AluOpType.add

P = 128
POSITIONS = 512
K = 2048
HEAD = 128
PAIRS = HEAD // 2
Q_HEADS, K_HEADS, V_HEADS = 16, 4, 4

K_PASS = 4 * P
PASSES = K // K_PASS
WORDS = K_PASS // 2

SLAB = 256
SLAB_TILES = SLAB // P
SLAB_HEADS = SLAB // HEAD
TILES = POSITIONS // P
X_SLABS = POSITIONS // SLAB
W_SLABS = (Q_HEADS + K_HEADS + V_HEADS) // SLAB_HEADS
ROTATED_SLABS = (Q_HEADS + K_HEADS) // SLAB_HEADS
RAW_SLABS_IN_SBUF = 8

FLOPS = 2 * POSITIONS * K * (Q_HEADS + K_HEADS + V_HEADS) * HEAD


def tile_rlaattention_pa_kernel(tc, x, freqs_cis, Wqkv, out_0, out_1, out_2):
    nc = tc.nc

    x_rows = x.flatten_outer_dims().rearrange("(p i) k -> p i k", i=TILES)
    freq_rows = freqs_cis.rearrange("(p i) d -> p i d", i=TILES)
    slab_rows = [
        out.rearrange("b h (p i) d -> p (b h) i d", i=TILES)[:, h : h + SLAB_HEADS]
        for out, heads in ((out_0, Q_HEADS), (out_1, K_HEADS), (out_2, V_HEADS))
        for h in range(0, heads, SLAB_HEADS)
    ]

    with ExitStack() as ctx:
        ctx.enter_context(tc.manual_schedule())
        keep = ctx.enter_context(tc.tile_pool(name="keep", bufs=1))
        raw_pool = ctx.enter_context(tc.tile_pool(name="raw", bufs=RAW_SLABS_IN_SBUF))
        stage = ctx.enter_context(tc.tile_pool(name="stage", bufs=2 * PASSES))
        w_mx = ctx.enter_context(tc.tile_pool(name="w_mx", bufs=3))
        products = ctx.enter_context(tc.tile_pool(name="products", bufs=3))
        results = ctx.enter_context(tc.tile_pool(name="results", bufs=8))
        flipped_banks = ctx.enter_context(tc.psum_pool(name="flipped_banks", bufs=4))
        sum_banks = ctx.enter_context(tc.psum_pool(name="sum_banks", bufs=4))

        def load_w_slab(s):
            w_raw = raw_pool.tile([P, SLAB_TILES, K], BF16, tag="w_raw")
            nc.sync.dma_start(
                out=w_raw[:],
                in_=Wqkv[SLAB * s : SLAB * (s + 1), :].rearrange("(r p) k -> p r k", p=P),
            )
            return w_raw

        def flip_slab(raw, vector_helps):
            grouped_tiles = []
            for c in range(PASSES):
                flipped = flipped_banks.tile([P, 2, SLAB], F32, tag="flipped")
                for u in range(2):
                    for r in range(SLAB_TILES):
                        first_word = WORDS * c + P * u
                        nc.tensor.transpose(
                            flipped[:, u, P * r : P * (r + 1)],
                            raw[:, r, :].bitcast(F32)[:, first_word : first_word + P],
                            identity[:],
                        )
                grouped = stage.tile([P, 4 * SLAB], BF16, tag="grouped", align_bytes=64)
                side_by_side = grouped[:].bitcast(F32).rearrange("p (n u) -> p n u", u=2)
                planes = flipped[:].rearrange("p u n -> p n u")
                if vector_helps and c == 1:
                    nc.vector.tensor_copy(out=side_by_side, in_=planes)
                else:
                    nc.scalar.copy(out=side_by_side, in_=planes)
                grouped_tiles.append(grouped)
            return grouped_tiles

        def quantise_slab(grouped_tiles, codes, scales):
            for c in range(PASSES):
                nc.vector.quantize_mx(
                    out=codes[:, c, :].bitcast(FP8X4),
                    scales=scales[:, c, :],
                    in_=grouped_tiles[c][:],
                )

        freq_raw = keep.tile([P, TILES, PAIRS, 2], BF16)
        nc.scalar.dma_start(
            out=freq_raw[:].rearrange("p i j e -> p i (j e)"), in_=freq_rows
        )
        x_raws = []
        for s in range(X_SLABS):
            x_raw = keep.tile([P, SLAB_TILES, K], BF16, name="x_raw%d" % s)
            nc.sync.dma_start(
                out=x_raw[:], in_=x_rows[:, SLAB_TILES * s : SLAB_TILES * (s + 1), :]
            )
            x_raws.append(x_raw)
        w_raws = [load_w_slab(s) for s in range(RAW_SLABS_IN_SBUF)]

        identity = keep.tile([P, P], F32)
        make_identity(nc, identity[:])

        for_even = keep.tile([P, TILES, PAIRS, 2], F32)
        for_odd = keep.tile([P, TILES, PAIRS, 2], F32)
        nc.vector.tensor_copy(out=for_even[:, :, :, 0], in_=freq_raw[:, :, :, 1])
        nc.vector.tensor_copy(out=for_even[:, :, :, 1], in_=freq_raw[:, :, :, 0])
        nc.vector.tensor_scalar_mul(for_odd[:, :, :, 0], freq_raw[:, :, :, 0], -1.0)
        nc.vector.tensor_copy(out=for_odd[:, :, :, 1], in_=freq_raw[:, :, :, 1])

        x_codes = keep.tile([P, PASSES, POSITIONS], U32, align_bytes=64)
        x_scales = keep.tile([P, PASSES, POSITIONS], U8, align_bytes=64)
        for s in range(X_SLABS):
            columns = slice(SLAB * s, SLAB * (s + 1))
            quantise_slab(
                flip_slab(x_raws[s], True), x_codes[:, :, columns], x_scales[:, :, columns]
            )

        w_grouped = []
        w_quantised = []

        def flip_w_slab(s):
            w_grouped.append(flip_slab(w_raws[s], s < 2))
            if s + RAW_SLABS_IN_SBUF < W_SLABS:
                w_raws.append(load_w_slab(s + RAW_SLABS_IN_SBUF))

        def quantise_w_slab(s):
            w_codes = w_mx.tile([P, PASSES, SLAB], U32, tag="w_codes", align_bytes=64)
            w_scales = w_mx.tile([P, PASSES, SLAB], U8, tag="w_scales", align_bytes=64)
            quantise_slab(w_grouped[s], w_codes, w_scales)
            w_quantised.append((w_codes, w_scales))

        def multiply_slab(s, first_tile):
            w_codes, w_scales = w_quantised[s]
            sums = sum_banks.tile([P, 2, SLAB], F32, tag="sums")
            for t in range(2):
                positions = slice(P * (first_tile + t), P * (first_tile + t + 1))
                for c in range(PASSES):
                    nc.tensor.matmul_mx(
                        out=sums[:, t, :],
                        lhsT=x_codes[:, c, positions].bitcast(FP8X4),
                        lhsT_scale=x_scales[:, c, positions],
                        rhs=w_codes[:, c, :].bitcast(FP8X4),
                        rhs_scale=w_scales[:, c, :],
                        start=(c == 0),
                        stop=(c == PASSES - 1),
                    )
            return sums

        flip_w_slab(0)
        quantise_w_slab(0)
        flip_w_slab(1)
        by_member = [P, 2, SLAB_HEADS, PAIRS, 2]
        for s in range(W_SLABS):
            if s + 2 < W_SLABS:
                flip_w_slab(s + 2)
            if s + 1 < W_SLABS:
                quantise_w_slab(s + 1)

            if s < ROTATED_SLABS:
                from_even = products.tile([P, TILES, SLAB_HEADS, PAIRS, 2], F32, tag="from_even")
                from_odd = products.tile([P, TILES, SLAB_HEADS, PAIRS, 2], F32, tag="from_odd")
                for first_tile in range(0, TILES, 2):
                    sums = multiply_slab(s, first_tile)
                    members = sums[:].rearrange(
                        "p t (h j e) -> p t h j e", h=SLAB_HEADS, e=2
                    )
                    tiles = slice(first_tile, first_tile + 2)
                    nc.vector.tensor_tensor(
                        out=from_even[:, tiles],
                        in0=members[:, :, :, :, 0:1].to_broadcast(by_member),
                        in1=for_even[:, tiles].unsqueeze(2).to_broadcast(by_member),
                        op=MULT,
                    )
                    nc.vector.tensor_tensor(
                        out=from_odd[:, tiles],
                        in0=members[:, :, :, :, 1:2].to_broadcast(by_member),
                        in1=for_odd[:, tiles].unsqueeze(2).to_broadcast(by_member),
                        op=MULT,
                    )
                result = results.tile([P, SLAB_HEADS, TILES, HEAD], F32, tag="result")
                nc.gpsimd.tensor_tensor(
                    out=result[:].rearrange("p h i d -> p i h d"),
                    in0=from_even[:].rearrange("p i h j e -> p i h (j e)"),
                    in1=from_odd[:].rearrange("p i h j e -> p i h (j e)"),
                    op=ADD,
                )
                nc.sync.dma_start(out=slab_rows[s], in_=result[:])
            else:
                for first_tile in range(0, TILES, 2):
                    sums = multiply_slab(s, first_tile)
                    values = results.tile([P, SLAB_HEADS, 2, HEAD], F32, tag="values")
                    nc.scalar.copy(
                        out=values[:].rearrange("p h t d -> p t h d"),
                        in_=sums[:].rearrange("p t (h d) -> p t h d", h=SLAB_HEADS),
                    )
                    nc.scalar.dma_start(
                        out=slab_rows[s][:, :, first_tile : first_tile + 2, :], in_=values[:]
                    )
